import numpy as np
import ml_dtypes

BF16 = ml_dtypes.bfloat16


def bf(x):
    return np.asarray(x, np.float32).astype(BF16)


def f32(x):
    return np.asarray(x, np.float32)


def f64(x):
    return np.asarray(x).astype(np.float64)


def striped(idx):
    return np.tile(idx.reshape(-1, 16).T, (8, 1))


DIM, C, M, S, N, T, R, H = 128, 256, 1024, 512, 64, 256, 4, 2
EPS = 1e-6


def sigmoid(v):
    return 1.0 / (1.0 + np.exp(-v))


def setup_inputs():
    return {"x": bf(np.random.standard_normal((DIM, T))), "w": bf(np.random.standard_normal((DIM, M)) / np.sqrt(DIM)), "ape": f32(0.5 * np.random.standard_normal((C, R * H))), "norm_weight": f32(1.0 + 0.1 * np.random.standard_normal((C, 1))), "base": f32(np.random.standard_normal((C, S))), "offs": striped(np.random.permutation(S)[:N])}


def reference(x, w, ape, norm_weight, base, offs):
    idx = offs[:16].T.reshape(-1)
    sc = f64(w).T @ f64(x)
    u = sc[:H * C] * sigmoid(sc[H * C:])
    a = f64(ape)
    cur = u[:C].reshape(C, N, R)
    prv = u[C:].reshape(C, N, R)
    comp = (cur * a[:, None, :R]).sum(axis=-1)
    comp[:, 1:] = comp[:, 1:] + (prv[:, :-1] * a[:, None, R:]).sum(axis=-1)
    rms = 1.0 / np.sqrt((comp * comp).mean(axis=0, keepdims=True) + EPS)
    res = f64(base).copy()
    res[:, idx] = comp * rms * f64(norm_weight)
    return res

@@ -1,0 +1,108 @@
+import concourse.mybir as mybir
+
+F32 = mybir.dt.float32
+BF16 = mybir.dt.bfloat16
+U16 = mybir.dt.uint16
+MULT = mybir.AluOpType.mult
+ADD = mybir.AluOpType.add
+SIGMOID = mybir.ActivationFunctionType.Sigmoid
+SQRT = mybir.ActivationFunctionType.Sqrt
+
+P = 128
+DIM = 128
+C = 256
+T = 256
+R = 4
+H = 2
+N = T // R
+SLOTS = 512
+BLOCKS = C // P
+EPS = 1e-6
+
+FLOPS = 2 * DIM * (2 * H * C) * T
+
+
+def tile_compressor_kernel(tc, x, w, ape, norm_weight, base, offs, out):
+    nc = tc.nc
+    with (
+        tc.tile_pool(name="held", bufs=1) as held,
+        tc.psum_pool(name="psum", bufs=1) as psum,
+    ):
+        x_sb = held.tile([P, T], BF16, name="x_sb")
+        w_gate = held.tile([P, H * C], BF16, name="w_gate")
+        w_val = held.tile([P, H * C], BF16, name="w_val")
+        offsets = held.tile([P, N // 16], U16, name="offsets")
+        nc.sync.dma_start(x_sb[:], x)
+        nc.scalar.dma_start(w_gate[:], w[:, H * C : 2 * H * C])
+        nc.sync.dma_start(w_val[:], w[:, 0 : H * C])
+        nc.sync.dma_start(offsets[:], offs)
+
+        ape_sb = [held.tile([P, H * R], F32, name=f"ape_sb{b}") for b in range(BLOCKS)]
+        gain = [held.tile([P, 1], F32, name=f"gain{b}") for b in range(BLOCKS)]
+        window = [held.tile([P, SLOTS], F32, name=f"window{b}") for b in range(BLOCKS)]
+        for b in range(BLOCKS):
+            rows = slice(b * P, (b + 1) * P)
+            nc.gpsimd.dma_start(ape_sb[b][:], ape[rows, :])
+            nc.gpsimd.dma_start(gain[b][:], norm_weight[rows, :])
+        nc.sync.dma_start(window[0][:], base[0:P, :])
+        nc.scalar.dma_start(window[1][:], base[P : 2 * P, :])
+
+        ones = held.tile([P, P], F32, name="ones")
+        nc.gpsimd.memset(ones[:], 1.0)
+
+        x_by_place = x_sb[:].rearrange("k (j r) -> k r j", r=R)
+
+        square_sum = psum.tile([P, N], F32, name="square_sum")
+        scaled = []
+        for b in range(BLOCKS):
+            gate_ps = psum.tile([P, H * T], F32, name=f"gate_ps{b}")
+            val_ps = psum.tile([P, H * T], F32, name=f"val_ps{b}")
+            for bank, weights in ((gate_ps, w_gate), (val_ps, w_val)):
+                for h in range(H):
+                    nc.tensor.matmul(
+                        bank[:, h * T : (h + 1) * T].rearrange("p (r j) -> p r j", r=R),
+                        weights[:, h * C + b * P : h * C + (b + 1) * P],
+                        x_by_place,
+                        start=True,
+                        stop=True,
+                    )
+
+            sig = held.tile([P, H * T], F32, name=f"sig{b}")
+            nc.scalar.activation(sig[:], gate_ps[:], SIGMOID)
+
+            terms = held.tile([P, H * R, N], F32, name=f"terms{b}")
+            nc.vector.memset(terms[:, R : H * R, 0:1], 0.0)
+            for k in range(H * R):
+                shift = k // R
+                src = slice(k * N, (k + 1) * N - shift)
+                nc.vector.scalar_tensor_tensor(
+                    out=terms[:, k, shift:N],
+                    in0=val_ps[:, src],
+                    scalar=ape_sb[b][:, k : k + 1],
+                    in1=sig[:, src],
+                    op0=MULT,
+                    op1=MULT,
+                )
+            comp = held.tile([P, N], F32, name=f"comp{b}")
+            nc.vector.tensor_reduce(
+                out=comp[:], in_=terms[:].rearrange("p k j -> p j k"), axis=mybir.AxisListType.X, op=ADD
+            )
+
+            squares = held.tile([P, N], F32, name=f"squares{b}")
+            nc.vector.tensor_tensor(squares[:], comp[:], comp[:], MULT)
+            nc.tensor.matmul(square_sum[:], ones[:], squares[:], start=(b == 0), stop=(b == BLOCKS - 1))
+
+            comp_gain = held.tile([P, N], F32, name=f"comp_gain{b}")
+            nc.vector.tensor_scalar(
+                out=comp_gain[:], in0=comp[:], scalar1=gain[b][:, 0:1], scalar2=None, op0=MULT
+            )
+            scaled.append(comp_gain)
+
+        root = held.tile([P, N], F32, name="root")
+        nc.scalar.activation(root[:], square_sum[:], SQRT, bias=EPS, scale=1.0 / C)
+        rms = held.tile([P, N], F32, name="rms")
+        nc.vector.reciprocal(rms[:], root[:])
+
+        for b, queue in zip(range(BLOCKS), (nc.sync, nc.scalar)):
+            nc.vector.tensor_tensor(window[b][:].indirect(offsets[:]), scaled[b][:], rms[:], MULT)
+            queue.dma_start(out[b * P : (b + 1) * P, :], window[b][:])

@@ -32,18 +32,15 @@ def tile_compressor_kernel(tc, x, w, ape, norm_weight, base, offs, out):
         w_gate = held.tile([P, H * C], BF16, name="w_gate")
         w_val = held.tile([P, H * C], BF16, name="w_val")
         offsets = held.tile([P, N // 16], U16, name="offsets")
+        ape_sb = held.tile([P, BLOCKS, H * R], F32, name="ape_sb")
+        gain = held.tile([P, BLOCKS, 1], F32, name="gain")
+        window = [held.tile([P, SLOTS], F32, name=f"window{b}") for b in range(BLOCKS)]
         nc.sync.dma_start(x_sb[:], x)
         nc.scalar.dma_start(w_gate[:], w[:, H * C : 2 * H * C])
+        nc.sync.dma_start(ape_sb[:], ape.rearrange("(b p) k -> p b k", p=P))
         nc.sync.dma_start(w_val[:], w[:, 0 : H * C])
+        nc.scalar.dma_start(gain[:], norm_weight.rearrange("(b p) o -> p b o", p=P))
         nc.sync.dma_start(offsets[:], offs)
-
-        ape_sb = [held.tile([P, H * R], F32, name=f"ape_sb{b}") for b in range(BLOCKS)]
-        gain = [held.tile([P, 1], F32, name=f"gain{b}") for b in range(BLOCKS)]
-        window = [held.tile([P, SLOTS], F32, name=f"window{b}") for b in range(BLOCKS)]
-        for b in range(BLOCKS):
-            rows = slice(b * P, (b + 1) * P)
-            nc.gpsimd.dma_start(ape_sb[b][:], ape[rows, :])
-            nc.gpsimd.dma_start(gain[b][:], norm_weight[rows, :])
         nc.sync.dma_start(window[0][:], base[0:P, :])
         nc.scalar.dma_start(window[1][:], base[P : 2 * P, :])
 
@@ -78,7 +75,7 @@ def tile_compressor_kernel(tc, x, w, ape, norm_weight, base, offs, out):
                 nc.vector.scalar_tensor_tensor(
                     out=terms[:, k, shift:N],
                     in0=val_ps[:, src],
-                    scalar=ape_sb[b][:, k : k + 1],
+                    scalar=ape_sb[:, b, k : k + 1],
                     in1=sig[:, src],
                     op0=MULT,
                     op1=MULT,
@@ -94,7 +91,7 @@ def tile_compressor_kernel(tc, x, w, ape, norm_weight, base, offs, out):
 
             comp_gain = held.tile([P, N], F32, name=f"comp_gain{b}")
             nc.vector.tensor_scalar(
-                out=comp_gain[:], in0=comp[:], scalar1=gain[b][:, 0:1], scalar2=None, op0=MULT
+                out=comp_gain[:], in0=comp[:], scalar1=gain[:, b, :], scalar2=None, op0=MULT
             )
             scaled.append(comp_gain)
 

@@ -26,7 +26,9 @@ def tile_compressor_kernel(tc, x, w, ape, norm_weight, base, offs, out):
     nc = tc.nc
     with (
         tc.tile_pool(name="held", bufs=1) as held,
-        tc.psum_pool(name="psum", bufs=1) as psum,
+        tc.psum_pool(name="gate_banks", bufs=3) as gate_banks,
+        tc.psum_pool(name="val_banks", bufs=BLOCKS * H) as val_banks,
+        tc.psum_pool(name="sum_bank", bufs=1) as sum_bank,
     ):
         x_sb = held.tile([P, T], BF16, name="x_sb")
         w_gate = held.tile([P, H * C], BF16, name="w_gate")
@@ -37,66 +39,66 @@ def tile_compressor_kernel(tc, x, w, ape, norm_weight, base, offs, out):
         window = [held.tile([P, SLOTS], F32, name=f"window{b}") for b in range(BLOCKS)]
         nc.sync.dma_start(x_sb[:], x)
         nc.scalar.dma_start(w_gate[:], w[:, H * C : 2 * H * C])
-        nc.sync.dma_start(ape_sb[:], ape.rearrange("(b p) k -> p b k", p=P))
         nc.sync.dma_start(w_val[:], w[:, 0 : H * C])
+        nc.scalar.dma_start(ape_sb[:], ape.rearrange("(b p) k -> p b k", p=P))
         nc.scalar.dma_start(gain[:], norm_weight.rearrange("(b p) o -> p b o", p=P))
         nc.sync.dma_start(offsets[:], offs)
-        nc.sync.dma_start(window[0][:], base[0:P, :])
-        nc.scalar.dma_start(window[1][:], base[P : 2 * P, :])
+        for b in range(BLOCKS):
+            nc.sync.dma_start(window[b][:], base[b * P : (b + 1) * P, :])
 
         ones = held.tile([P, P], F32, name="ones")
         nc.gpsimd.memset(ones[:], 1.0)
 
         x_by_place = x_sb[:].rearrange("k (j r) -> k r j", r=R)
 
-        square_sum = psum.tile([P, N], F32, name="square_sum")
-        scaled = []
+        square_sum = sum_bank.tile([P, N], F32, name="square_sum")
+        comp = []
         for b in range(BLOCKS):
-            gate_ps = psum.tile([P, H * T], F32, name=f"gate_ps{b}")
-            val_ps = psum.tile([P, H * T], F32, name=f"val_ps{b}")
-            for bank, weights in ((gate_ps, w_gate), (val_ps, w_val)):
-                for h in range(H):
+            terms = held.tile([P, H * R, N], F32, name=f"terms{b}")
+            nc.vector.memset(terms[:, R : H * R, 0:1], 0.0)
+            for h in range(H):
+                columns = slice(h * C + b * P, h * C + (b + 1) * P)
+                gate_ps = gate_banks.tile([P, T], F32, name="gate_ps")
+                val_ps = val_banks.tile([P, T], F32, name="val_ps")
+                for bank, weights in ((gate_ps, w_gate), (val_ps, w_val)):
                     nc.tensor.matmul(
-                        bank[:, h * T : (h + 1) * T].rearrange("p (r j) -> p r j", r=R),
-                        weights[:, h * C + b * P : h * C + (b + 1) * P],
+                        bank[:].rearrange("p (r j) -> p r j", r=R),
+                        weights[:, columns],
                         x_by_place,
                         start=True,
                         stop=True,
                     )
-
-            sig = held.tile([P, H * T], F32, name=f"sig{b}")
-            nc.scalar.activation(sig[:], gate_ps[:], SIGMOID)
-
-            terms = held.tile([P, H * R, N], F32, name=f"terms{b}")
-            nc.vector.memset(terms[:, R : H * R, 0:1], 0.0)
-            for k in range(H * R):
-                shift = k // R
-                src = slice(k * N, (k + 1) * N - shift)
-                nc.vector.scalar_tensor_tensor(
-                    out=terms[:, k, shift:N],
-                    in0=val_ps[:, src],
-                    scalar=ape_sb[:, b, k : k + 1],
-                    in1=sig[:, src],
-                    op0=MULT,
-                    op1=MULT,
-                )
-            comp = held.tile([P, N], F32, name=f"comp{b}")
+                sig = held.tile([P, T], F32, name=f"sig{b}{h}")
+                nc.scalar.activation(sig[:], gate_ps[:], SIGMOID)
+                for r in range(R):
+                    src = slice(r * N, (r + 1) * N - h)
+                    nc.vector.scalar_tensor_tensor(
+                        out=terms[:, h * R + r, h:N],
+                        in0=val_ps[:, src],
+                        scalar=ape_sb[:, b, h * R + r : h * R + r + 1],
+                        in1=sig[:, src],
+                        op0=MULT,
+                        op1=MULT,
+                    )
+            comp_b = held.tile([P, N], F32, name=f"comp{b}")
             nc.vector.tensor_reduce(
-                out=comp[:], in_=terms[:].rearrange("p k j -> p j k"), axis=mybir.AxisListType.X, op=ADD
+                out=comp_b[:], in_=terms[:].rearrange("p k j -> p j k"), axis=mybir.AxisListType.X, op=ADD
             )
+            comp.append(comp_b)
 
             squares = held.tile([P, N], F32, name=f"squares{b}")
-            nc.vector.tensor_tensor(squares[:], comp[:], comp[:], MULT)
+            nc.vector.tensor_tensor(squares[:], comp_b[:], comp_b[:], MULT)
             nc.tensor.matmul(square_sum[:], ones[:], squares[:], start=(b == 0), stop=(b == BLOCKS - 1))
-
-            comp_gain = held.tile([P, N], F32, name=f"comp_gain{b}")
-            nc.vector.tensor_scalar(
-                out=comp_gain[:], in0=comp[:], scalar1=gain[:, b, :], scalar2=None, op0=MULT
-            )
-            scaled.append(comp_gain)
 
         root = held.tile([P, N], F32, name="root")
         nc.scalar.activation(root[:], square_sum[:], SQRT, bias=EPS, scale=1.0 / C)
+
+        scaled = []
+        for b in range(BLOCKS):
+            comp_gain = held.tile([P, N], F32, name=f"comp_gain{b}")
+            nc.vector.tensor_scalar(out=comp_gain[:], in0=comp[b][:], scalar1=gain[:, b, :], scalar2=None, op0=MULT)
+            scaled.append(comp_gain)
+
         rms = held.tile([P, N], F32, name="rms")
         nc.vector.reciprocal(rms[:], root[:])
 

@@ -51,11 +51,9 @@ def tile_compressor_kernel(tc, x, w, ape, norm_weight, base, offs, out):
 
         x_by_place = x_sb[:].rearrange("k (j r) -> k r j", r=R)
 
-        square_sum = sum_bank.tile([P, N], F32, name="square_sum")
-        comp = []
+        terms = held.tile([P, H * R, BLOCKS, N], F32, name="terms")
+        nc.vector.memset(terms[:, R : H * R, :, 0:1], 0.0)
         for b in range(BLOCKS):
-            terms = held.tile([P, H * R, N], F32, name=f"terms{b}")
-            nc.vector.memset(terms[:, R : H * R, 0:1], 0.0)
             for h in range(H):
                 columns = slice(h * C + b * P, h * C + (b + 1) * P)
                 gate_ps = gate_banks.tile([P, T], F32, name="gate_ps")
@@ -73,22 +71,26 @@ def tile_compressor_kernel(tc, x, w, ape, norm_weight, base, offs, out):
                 for r in range(R):
                     src = slice(r * N, (r + 1) * N - h)
                     nc.vector.scalar_tensor_tensor(
-                        out=terms[:, h * R + r, h:N],
+                        out=terms[:, h * R + r, b, h:N],
                         in0=val_ps[:, src],
                         scalar=ape_sb[:, b, h * R + r : h * R + r + 1],
                         in1=sig[:, src],
                         op0=MULT,
                         op1=MULT,
                     )
-            comp_b = held.tile([P, N], F32, name=f"comp{b}")
-            nc.vector.tensor_reduce(
-                out=comp_b[:], in_=terms[:].rearrange("p k j -> p j k"), axis=mybir.AxisListType.X, op=ADD
-            )
-            comp.append(comp_b)
 
-            squares = held.tile([P, N], F32, name=f"squares{b}")
-            nc.vector.tensor_tensor(squares[:], comp_b[:], comp_b[:], MULT)
-            nc.tensor.matmul(square_sum[:], ones[:], squares[:], start=(b == 0), stop=(b == BLOCKS - 1))
+        sum4 = held.tile([P, 4, BLOCKS, N], F32, name="sum4")
+        sum2 = held.tile([P, 2, BLOCKS, N], F32, name="sum2")
+        comp = held.tile([P, BLOCKS, N], F32, name="comp")
+        nc.vector.tensor_tensor(sum4[:], terms[:, 0:4], terms[:, 4:8], ADD)
+        nc.vector.tensor_tensor(sum2[:], sum4[:, 0:2], sum4[:, 2:4], ADD)
+        nc.vector.tensor_tensor(comp[:], sum2[:, 0], sum2[:, 1], ADD)
+
+        squares = held.tile([P, BLOCKS, N], F32, name="squares")
+        nc.vector.tensor_tensor(squares[:], comp[:], comp[:], MULT)
+        square_sum = sum_bank.tile([P, N], F32, name="square_sum")
+        for b in range(BLOCKS):
+            nc.tensor.matmul(square_sum[:], ones[:], squares[:, b, :], start=(b == 0), stop=(b == BLOCKS - 1))
 
         root = held.tile([P, N], F32, name="root")
         nc.scalar.activation(root[:], square_sum[:], SQRT, bias=EPS, scale=1.0 / C)
@@ -96,7 +98,7 @@ def tile_compressor_kernel(tc, x, w, ape, norm_weight, base, offs, out):
         scaled = []
         for b in range(BLOCKS):
             comp_gain = held.tile([P, N], F32, name=f"comp_gain{b}")
-            nc.vector.tensor_scalar(out=comp_gain[:], in0=comp[b][:], scalar1=gain[:, b, :], scalar2=None, op0=MULT)
+            nc.vector.tensor_scalar(out=comp_gain[:], in0=comp[:, b, :], scalar1=gain[:, b, :], scalar2=None, op0=MULT)
             scaled.append(comp_gain)
 
         rms = held.tile([P, N], F32, name="rms")

@@ -18,6 +18,8 @@ N = T // R
 SLOTS = 512
 BLOCKS = C // P
 EPS = 1e-6
+PSUM_BANKS = 8
+WARM_UPS = 6
 
 FLOPS = 2 * DIM * (2 * H * C) * T
 
@@ -26,9 +28,7 @@ def tile_compressor_kernel(tc, x, w, ape, norm_weight, base, offs, out):
     nc = tc.nc
     with (
         tc.tile_pool(name="held", bufs=1) as held,
-        tc.psum_pool(name="gate_banks", bufs=3) as gate_banks,
-        tc.psum_pool(name="val_banks", bufs=BLOCKS * H) as val_banks,
-        tc.psum_pool(name="sum_bank", bufs=1) as sum_bank,
+        tc.psum_pool(name="banks", bufs=PSUM_BANKS) as banks,
     ):
         x_sb = held.tile([P, T], BF16, name="x_sb")
         w_gate = held.tile([P, H * C], BF16, name="w_gate")
@@ -46,18 +46,26 @@ def tile_compressor_kernel(tc, x, w, ape, norm_weight, base, offs, out):
         for b in range(BLOCKS):
             nc.sync.dma_start(window[b][:], base[b * P : (b + 1) * P, :])
 
+        zeros = held.tile([P, T], BF16, name="zeros")
+        nc.gpsimd.memset(zeros[:], 0.0)
+        warm_ps = banks.tile([P, T], F32, name="warm_ps", tag="bank")
+        for repeat in range(WARM_UPS):
+            nc.tensor.matmul(warm_ps[:], zeros[:, 0:P], zeros[:], start=True, stop=True)
+
         ones = held.tile([P, P], F32, name="ones")
         nc.gpsimd.memset(ones[:], 1.0)
 
         x_by_place = x_sb[:].rearrange("k (j r) -> k r j", r=R)
 
-        terms = held.tile([P, H * R, BLOCKS, N], F32, name="terms")
-        nc.vector.memset(terms[:, R : H * R, :, 0:1], 0.0)
+        comp = []
+        squares = []
         for b in range(BLOCKS):
+            terms = held.tile([P, H * R, N], F32, name=f"terms{b}")
+            nc.vector.memset(terms[:, R : H * R, 0:1], 0.0)
             for h in range(H):
                 columns = slice(h * C + b * P, h * C + (b + 1) * P)
-                gate_ps = gate_banks.tile([P, T], F32, name="gate_ps")
-                val_ps = val_banks.tile([P, T], F32, name="val_ps")
+                gate_ps = banks.tile([P, T], F32, name="gate_ps", tag="bank")
+                val_ps = banks.tile([P, T], F32, name="val_ps", tag="bank")
                 for bank, weights in ((gate_ps, w_gate), (val_ps, w_val)):
                     nc.tensor.matmul(
                         bank[:].rearrange("p (r j) -> p r j", r=R),
@@ -71,26 +79,26 @@ def tile_compressor_kernel(tc, x, w, ape, norm_weight, base, offs, out):
                 for r in range(R):
                     src = slice(r * N, (r + 1) * N - h)
                     nc.vector.scalar_tensor_tensor(
-                        out=terms[:, h * R + r, b, h:N],
+                        out=terms[:, h * R + r, h:N],
                         in0=val_ps[:, src],
                         scalar=ape_sb[:, b, h * R + r : h * R + r + 1],
                         in1=sig[:, src],
                         op0=MULT,
                         op1=MULT,
                     )
+            comp_b = held.tile([P, N], F32, name=f"comp{b}")
+            nc.vector.tensor_reduce(
+                out=comp_b[:], in_=terms[:].rearrange("p k j -> p j k"), axis=mybir.AxisListType.X, op=ADD
+            )
+            comp.append(comp_b)
 
-        sum4 = held.tile([P, 4, BLOCKS, N], F32, name="sum4")
-        sum2 = held.tile([P, 2, BLOCKS, N], F32, name="sum2")
-        comp = held.tile([P, BLOCKS, N], F32, name="comp")
-        nc.vector.tensor_tensor(sum4[:], terms[:, 0:4], terms[:, 4:8], ADD)
-        nc.vector.tensor_tensor(sum2[:], sum4[:, 0:2], sum4[:, 2:4], ADD)
-        nc.vector.tensor_tensor(comp[:], sum2[:, 0], sum2[:, 1], ADD)
+            squares_b = held.tile([P, N], F32, name=f"squares{b}")
+            nc.vector.tensor_tensor(squares_b[:], comp_b[:], comp_b[:], MULT)
+            squares.append(squares_b)
 
-        squares = held.tile([P, BLOCKS, N], F32, name="squares")
-        nc.vector.tensor_tensor(squares[:], comp[:], comp[:], MULT)
-        square_sum = sum_bank.tile([P, N], F32, name="square_sum")
+        square_sum = banks.tile([P, N], F32, name="square_sum", tag="bank")
         for b in range(BLOCKS):
-            nc.tensor.matmul(square_sum[:], ones[:], squares[:, b, :], start=(b == 0), stop=(b == BLOCKS - 1))
+            nc.tensor.matmul(square_sum[:], ones[:], squares[b][:], start=(b == 0), stop=(b == BLOCKS - 1))
 
         root = held.tile([P, N], F32, name="root")
         nc.scalar.activation(root[:], square_sum[:], SQRT, bias=EPS, scale=1.0 / C)
@@ -98,7 +106,7 @@ def tile_compressor_kernel(tc, x, w, ape, norm_weight, base, offs, out):
         scaled = []
         for b in range(BLOCKS):
             comp_gain = held.tile([P, N], F32, name=f"comp_gain{b}")
-            nc.vector.tensor_scalar(out=comp_gain[:], in0=comp[:, b, :], scalar1=gain[:, b, :], scalar2=None, op0=MULT)
+            nc.vector.tensor_scalar(out=comp_gain[:], in0=comp[b][:], scalar1=gain[:, b, :], scalar2=None, op0=MULT)
             scaled.append(comp_gain)
 
         rms = held.tile([P, N], F32, name="rms")

@@ -6,7 +6,7 @@ U16 = mybir.dt.uint16
 MULT = mybir.AluOpType.mult
 ADD = mybir.AluOpType.add
 SIGMOID = mybir.ActivationFunctionType.Sigmoid
-SQRT = mybir.ActivationFunctionType.Sqrt
+RSQRT = mybir.ActivationFunctionType.Abs_reciprocal_sqrt
 
 P = 128
 DIM = 128
@@ -100,17 +100,14 @@ def tile_compressor_kernel(tc, x, w, ape, norm_weight, base, offs, out):
         for b in range(BLOCKS):
             nc.tensor.matmul(square_sum[:], ones[:], squares[b][:], start=(b == 0), stop=(b == BLOCKS - 1))
 
-        root = held.tile([P, N], F32, name="root")
-        nc.scalar.activation(root[:], square_sum[:], SQRT, bias=EPS, scale=1.0 / C)
+        rms = held.tile([P, N], F32, name="rms")
+        nc.scalar.activation(rms[:], square_sum[:], RSQRT, bias=EPS, scale=1.0 / C)
 
         scaled = []
         for b in range(BLOCKS):
             comp_gain = held.tile([P, N], F32, name=f"comp_gain{b}")
             nc.vector.tensor_scalar(out=comp_gain[:], in0=comp[b][:], scalar1=gain[:, b, :], scalar2=None, op0=MULT)
             scaled.append(comp_gain)
-
-        rms = held.tile([P, N], F32, name="rms")
-        nc.vector.reciprocal(rms[:], root[:])
 
         for b, queue in zip(range(BLOCKS), (nc.sync, nc.scalar)):
             nc.vector.tensor_tensor(window[b][:].indirect(offsets[:]), scaled[b][:], rms[:], MULT)

@@ -1,4 +1,5 @@
 import concourse.mybir as mybir
+from concourse.masks import make_identity
 
 F32 = mybir.dt.float32
 BF16 = mybir.dt.bfloat16
@@ -55,18 +56,19 @@ def tile_compressor_kernel(tc, x, w, ape, norm_weight, base, offs, out):
         ones = held.tile([P, P], F32, name="ones")
         nc.gpsimd.memset(ones[:], 1.0)
 
+        identity = held.tile([P, P], F32, name="identity")
+        make_identity(nc, identity[:])
+
         x_by_place = x_sb[:].rearrange("k (j r) -> k r j", r=R)
 
-        comp = []
-        squares = []
+        gate_ps = {}
+        val_ps = {}
         for b in range(BLOCKS):
-            terms = held.tile([P, H * R, N], F32, name=f"terms{b}")
-            nc.vector.memset(terms[:, R : H * R, 0:1], 0.0)
             for h in range(H):
                 columns = slice(h * C + b * P, h * C + (b + 1) * P)
-                gate_ps = banks.tile([P, T], F32, name="gate_ps", tag="bank")
-                val_ps = banks.tile([P, T], F32, name="val_ps", tag="bank")
-                for bank, weights in ((gate_ps, w_gate), (val_ps, w_val)):
+                gate_ps[b, h] = banks.tile([P, T], F32, name=f"gate_ps{b}{h}", tag="bank")
+                val_ps[b, h] = banks.tile([P, T], F32, name=f"val_ps{b}{h}", tag="bank")
+                for bank, weights in ((gate_ps[b, h], w_gate), (val_ps[b, h], w_val)):
                     nc.tensor.matmul(
                         bank[:].rearrange("p (r j) -> p r j", r=R),
                         weights[:, columns],
@@ -74,22 +76,38 @@ def tile_compressor_kernel(tc, x, w, ape, norm_weight, base, offs, out):
                         start=True,
                         stop=True,
                     )
+
+        comp = []
+        squares = []
+        for b in range(BLOCKS):
+            terms = held.tile([P, H * R, N], F32, name=f"terms{b}")
+            nc.vector.memset(terms[:, R : H * R, 0:1], 0.0)
+            on_tensor = b < BLOCKS - 1
+            if on_tensor:
+                comp_ps = banks.tile([P, N], F32, name="comp_ps", tag="bank")
+            for h in range(H):
                 sig = held.tile([P, T], F32, name=f"sig{b}{h}")
-                nc.scalar.activation(sig[:], gate_ps[:], SIGMOID)
+                nc.scalar.activation(sig[:], gate_ps[b, h][:], SIGMOID)
                 for r in range(R):
                     src = slice(r * N, (r + 1) * N - h)
                     nc.vector.scalar_tensor_tensor(
                         out=terms[:, h * R + r, h:N],
-                        in0=val_ps[:, src],
+                        in0=val_ps[b, h][:, src],
                         scalar=ape_sb[:, b, h * R + r : h * R + r + 1],
                         in1=sig[:, src],
                         op0=MULT,
                         op1=MULT,
                     )
+                    if on_tensor:
+                        k = h * R + r
+                        nc.tensor.matmul(comp_ps[:], identity[:], terms[:, k, :], start=(k == 0), stop=(k == H * R - 1))
             comp_b = held.tile([P, N], F32, name=f"comp{b}")
-            nc.vector.tensor_reduce(
-                out=comp_b[:], in_=terms[:].rearrange("p k j -> p j k"), axis=mybir.AxisListType.X, op=ADD
-            )
+            if on_tensor:
+                nc.vector.tensor_copy(comp_b[:], comp_ps[:])
+            else:
+                nc.vector.tensor_reduce(
+                    out=comp_b[:], in_=terms[:].rearrange("p k j -> p j k"), axis=mybir.AxisListType.X, op=ADD
+                )
             comp.append(comp_b)
 
             squares_b = held.tile([P, N], F32, name=f"squares{b}")

@@ -8,6 +8,7 @@ MULT = mybir.AluOpType.mult
 ADD = mybir.AluOpType.add
 SIGMOID = mybir.ActivationFunctionType.Sigmoid
 RSQRT = mybir.ActivationFunctionType.Abs_reciprocal_sqrt
+SQUARE = mybir.ActivationFunctionType.Square
 
 P = 128
 DIM = 128
@@ -101,18 +102,21 @@ def tile_compressor_kernel(tc, x, w, ape, norm_weight, base, offs, out):
                     if on_tensor:
                         k = h * R + r
                         nc.tensor.matmul(comp_ps[:], identity[:], terms[:, k, :], start=(k == 0), stop=(k == H * R - 1))
-            comp_b = held.tile([P, N], F32, name=f"comp{b}")
+            squares_b = held.tile([P, N], F32, name=f"squares{b}")
             if on_tensor:
-                nc.vector.tensor_copy(comp_b[:], comp_ps[:])
+                comp_b = comp_ps
+                nc.scalar.activation(squares_b[:], comp_b[:], SQUARE)
             else:
+                comp_b = held.tile([P, N], F32, name="comp_sb")
                 nc.vector.tensor_reduce(
                     out=comp_b[:], in_=terms[:].rearrange("p k j -> p j k"), axis=mybir.AxisListType.X, op=ADD
                 )
+                nc.vector.tensor_tensor(squares_b[:], comp_b[:], comp_b[:], MULT)
             comp.append(comp_b)
-
-            squares_b = held.tile([P, N], F32, name=f"squares{b}")
-            nc.vector.tensor_tensor(squares_b[:], comp_b[:], comp_b[:], MULT)
             squares.append(squares_b)
+
+        early_call = held.tile([P, 1], F32, name="early_call")
+        nc.scalar.activation(early_call[:], sig[:, 0:1], RSQRT, bias=1.0)
 
         square_sum = banks.tile([P, N], F32, name="square_sum", tag="bank")
         for b in range(BLOCKS):

@@ -21,7 +21,6 @@ SLOTS = 512
 BLOCKS = C // P
 EPS = 1e-6
 PSUM_BANKS = 8
-WARM_UPS = 6
 
 FLOPS = 2 * DIM * (2 * H * C) * T
 
@@ -47,12 +46,6 @@ def tile_compressor_kernel(tc, x, w, ape, norm_weight, base, offs, out):
         nc.sync.dma_start(offsets[:], offs)
         for b in range(BLOCKS):
             nc.sync.dma_start(window[b][:], base[b * P : (b + 1) * P, :])
-
-        zeros = held.tile([P, T], BF16, name="zeros")
-        nc.gpsimd.memset(zeros[:], 0.0)
-        warm_ps = banks.tile([P, T], F32, name="warm_ps", tag="bank")
-        for repeat in range(WARM_UPS):
-            nc.tensor.matmul(warm_ps[:], zeros[:, 0:P], zeros[:], start=True, stop=True)
 
         ones = held.tile([P, P], F32, name="ones")
         nc.gpsimd.memset(ones[:], 1.0)

@@ -55,21 +55,25 @@ def tile_compressor_kernel(tc, x, w, ape, norm_weight, base, offs, out):
 
         x_by_place = x_sb[:].rearrange("k (j r) -> k r j", r=R)
 
-        gate_ps = {}
-        val_ps = {}
-        for b in range(BLOCKS):
-            for h in range(H):
-                columns = slice(h * C + b * P, h * C + (b + 1) * P)
-                gate_ps[b, h] = banks.tile([P, T], F32, name=f"gate_ps{b}{h}", tag="bank")
-                val_ps[b, h] = banks.tile([P, T], F32, name=f"val_ps{b}{h}", tag="bank")
-                for bank, weights in ((gate_ps[b, h], w_gate), (val_ps[b, h], w_val)):
-                    nc.tensor.matmul(
-                        bank[:].rearrange("p (r j) -> p r j", r=R),
-                        weights[:, columns],
-                        x_by_place,
-                        start=True,
-                        stop=True,
-                    )
+        units = [(b, h) for b in range(BLOCKS) for h in range(H)]
+        gate_ps = {unit: banks.tile([P, T], F32, name=f"gate_ps{unit[0]}{unit[1]}", tag="bank") for unit in units}
+        val_ps = {unit: banks.tile([P, T], F32, name=f"val_ps{unit[0]}{unit[1]}", tag="bank") for unit in units}
+
+        def project(bank, weights, unit):
+            b, h = unit
+            nc.tensor.matmul(
+                bank[unit][:].rearrange("p (r j) -> p r j", r=R),
+                weights[:, h * C + b * P : h * C + (b + 1) * P],
+                x_by_place,
+                start=True,
+                stop=True,
+            )
+
+        project(gate_ps, w_gate, units[0])
+        for ahead, unit in zip(units[1:], units):
+            project(gate_ps, w_gate, ahead)
+            project(val_ps, w_val, unit)
+        project(val_ps, w_val, units[-1])
 
         comp = []
         squares = []

@@ -20,6 +20,7 @@ N = T // R
 SLOTS = 512
 BLOCKS = C // P
 EPS = 1e-6
+GATES_AHEAD = 2
 PSUM_BANKS = 8
 
 FLOPS = 2 * DIM * (2 * H * C) * T
@@ -69,11 +70,12 @@ def tile_compressor_kernel(tc, x, w, ape, norm_weight, base, offs, out):
                 stop=True,
             )
 
-        project(gate_ps, w_gate, units[0])
-        for ahead, unit in zip(units[1:], units):
-            project(gate_ps, w_gate, ahead)
+        for unit in units[:GATES_AHEAD]:
+            project(gate_ps, w_gate, unit)
+        for i, unit in enumerate(units):
+            if i + GATES_AHEAD < len(units):
+                project(gate_ps, w_gate, units[i + GATES_AHEAD])
             project(val_ps, w_val, unit)
-        project(val_ps, w_val, units[-1])
 
         comp = []
         squares = []

@@ -98,9 +98,15 @@ def tile_compressor_kernel(tc, x, w, ape, norm_weight, base, offs, out):
                         op0=MULT,
                         op1=MULT,
                     )
-                    if on_tensor:
-                        k = h * R + r
-                        nc.tensor.matmul(comp_ps[:], identity[:], terms[:, k, :], start=(k == 0), stop=(k == H * R - 1))
+                    if on_tensor and h == 1:
+                        nc.tensor.matmul(comp_ps[:], identity[:], terms[:, R + r, :], start=(r == 0), stop=False)
+                if on_tensor and h == 0:
+                    pairs = held.tile([P, R // 2, N], F32, name="pairs")
+                    nc.gpsimd.tensor_tensor(pairs[:], terms[:, 0 : R // 2, :], terms[:, R // 2 : R, :], ADD)
+                    current_sum = held.tile([P, N], F32, name="current_sum")
+                    nc.gpsimd.tensor_tensor(current_sum[:], pairs[:, 0, :], pairs[:, 1, :], ADD)
+            if on_tensor:
+                nc.tensor.matmul(comp_ps[:], identity[:], current_sum[:], start=False, stop=True)
             squares_b = held.tile([P, N], F32, name=f"squares{b}")
             if on_tensor:
                 comp_b = comp_ps

@@ -57,25 +57,26 @@ def tile_compressor_kernel(tc, x, w, ape, norm_weight, base, offs, out):
         x_by_place = x_sb[:].rearrange("k (j r) -> k r j", r=R)
 
         units = [(b, h) for b in range(BLOCKS) for h in range(H)]
-        gate_ps = {unit: banks.tile([P, T], F32, name=f"gate_ps{unit[0]}{unit[1]}", tag="bank") for unit in units}
-        val_ps = {unit: banks.tile([P, T], F32, name=f"val_ps{unit[0]}{unit[1]}", tag="bank") for unit in units}
-
-        def project(bank, weights, unit):
+        def project(name, weights, unit, places):
             b, h = unit
+            bank = banks.tile([P, len(places), N], F32, name=f"{name}{b}{h}{places[0]}", tag="bank")
             nc.tensor.matmul(
-                bank[unit][:].rearrange("p (r j) -> p r j", r=R),
+                bank[:],
                 weights[:, h * C + b * P : h * C + (b + 1) * P],
-                x_by_place,
+                x_by_place[:, places[0] : places[-1] + 1, :],
                 start=True,
                 stop=True,
             )
+            return bank
 
-        for unit in units[:GATES_AHEAD]:
-            project(gate_ps, w_gate, unit)
+        all_places = range(R)
+        halves = (range(0, R // 2), range(R // 2, R))
+        gate_ps = {unit: project("gate_ps", w_gate, unit, all_places) for unit in units[:GATES_AHEAD]}
+        val_ps = {}
         for i, unit in enumerate(units):
             if i + GATES_AHEAD < len(units):
-                project(gate_ps, w_gate, units[i + GATES_AHEAD])
-            project(val_ps, w_val, unit)
+                gate_ps[units[i + GATES_AHEAD]] = project("gate_ps", w_gate, units[i + GATES_AHEAD], all_places)
+            val_ps[unit] = [project("val_ps", w_val, unit, half) for half in halves]
 
         comp = []
         squares = []
@@ -86,27 +87,30 @@ def tile_compressor_kernel(tc, x, w, ape, norm_weight, base, offs, out):
             if on_tensor:
                 comp_ps = banks.tile([P, N], F32, name="comp_ps", tag="bank")
             for h in range(H):
-                sig = held.tile([P, T], F32, name=f"sig{b}{h}")
+                sig = held.tile([P, R, N], F32, name=f"sig{b}{h}")
                 nc.scalar.activation(sig[:], gate_ps[b, h][:], SIGMOID)
                 for r in range(R):
-                    src = slice(r * N, (r + 1) * N - h)
+                    half = val_ps[b, h][r // (R // 2)]
                     nc.vector.scalar_tensor_tensor(
                         out=terms[:, h * R + r, h:N],
-                        in0=val_ps[b, h][:, src],
+                        in0=half[:, r % (R // 2), 0 : N - h],
                         scalar=ape_sb[:, b, h * R + r : h * R + r + 1],
-                        in1=sig[:, src],
+                        in1=sig[:, r, 0 : N - h],
                         op0=MULT,
                         op1=MULT,
                     )
-                    if on_tensor and h == 1:
-                        nc.tensor.matmul(comp_ps[:], identity[:], terms[:, R + r, :], start=(r == 0), stop=False)
-                if on_tensor and h == 0:
-                    pairs = held.tile([P, R // 2, N], F32, name="pairs")
-                    nc.gpsimd.tensor_tensor(pairs[:], terms[:, 0 : R // 2, :], terms[:, R // 2 : R, :], ADD)
-                    current_sum = held.tile([P, N], F32, name="current_sum")
-                    nc.gpsimd.tensor_tensor(current_sum[:], pairs[:, 0, :], pairs[:, 1, :], ADD)
-            if on_tensor:
-                nc.tensor.matmul(comp_ps[:], identity[:], current_sum[:], start=False, stop=True)
+                if on_tensor:
+                    first, middle, end = h * R, h * R + R // 2, (h + 1) * R
+                    pairs = held.tile([P, R // 2, N], F32, name=f"pairs{h}")
+                    nc.gpsimd.tensor_tensor(pairs[:], terms[:, first:middle, :], terms[:, middle:end, :], ADD)
+                    for i in range(R // 2):
+                        nc.tensor.matmul(
+                            comp_ps[:],
+                            identity[:],
+                            pairs[:, i, :],
+                            start=(h == 0 and i == 0),
+                            stop=(h == H - 1 and i == R // 2 - 1),
+                        )
             squares_b = held.tile([P, N], F32, name=f"squares{b}")
             if on_tensor:
                 comp_b = comp_ps
@@ -121,7 +125,7 @@ def tile_compressor_kernel(tc, x, w, ape, norm_weight, base, offs, out):
             squares.append(squares_b)
 
         early_call = held.tile([P, 1], F32, name="early_call")
-        nc.scalar.activation(early_call[:], sig[:, 0:1], RSQRT, bias=1.0)
+        nc.scalar.activation(early_call[:], sig[:, 0, 0:1], RSQRT, bias=1.0)
 
         square_sum = banks.tile([P, N], F32, name="square_sum", tag="bank")
         for b in range(BLOCKS):

@@ -117,9 +117,15 @@ def tile_compressor_kernel(tc, x, w, ape, norm_weight, base, offs, out):
                 nc.scalar.activation(squares_b[:], comp_b[:], SQUARE)
             else:
                 comp_b = held.tile([P, N], F32, name="comp_sb")
-                nc.vector.tensor_reduce(
-                    out=comp_b[:], in_=terms[:].rearrange("p k j -> p j k"), axis=mybir.AxisListType.X, op=ADD
-                )
+                places = held.tile([P, R, N], F32, name="places")
+                for half in halves:
+                    first, end = half[0], half[-1] + 1
+                    nc.vector.tensor_tensor(
+                        places[:, first:end, :], terms[:, first:end, :], terms[:, R + first : R + end, :], ADD
+                    )
+                two = held.tile([P, R // 2, N], F32, name="two")
+                nc.vector.tensor_tensor(two[:], places[:, 0 : R // 2, :], places[:, R // 2 : R, :], ADD)
+                nc.vector.tensor_tensor(comp_b[:], two[:, 0, :], two[:, 1, :], ADD)
                 nc.vector.tensor_tensor(squares_b[:], comp_b[:], comp_b[:], MULT)
             comp.append(comp_b)
             squares.append(squares_b)

import concourse.mybir as mybir
from concourse.masks import make_identity

F32 = mybir.dt.float32
BF16 = mybir.dt.bfloat16
U16 = mybir.dt.uint16
MULT = mybir.AluOpType.mult
ADD = mybir.AluOpType.add
SIGMOID = mybir.ActivationFunctionType.Sigmoid
RSQRT = mybir.ActivationFunctionType.Abs_reciprocal_sqrt
SQUARE = mybir.ActivationFunctionType.Square

P = 128
DIM = 128
C = 256
T = 256
R = 4
H = 2
N = T // R
SLOTS = 512
BLOCKS = C // P
EPS = 1e-6
GATES_AHEAD = 2
PSUM_BANKS = 8

FLOPS = 2 * DIM * (2 * H * C) * T


def tile_compressor_kernel(tc, x, w, ape, norm_weight, base, offs, out):
    nc = tc.nc
    with (
        tc.tile_pool(name="held", bufs=1) as held,
        tc.psum_pool(name="banks", bufs=PSUM_BANKS) as banks,
    ):
        x_sb = held.tile([P, T], BF16, name="x_sb")
        w_gate = held.tile([P, H * C], BF16, name="w_gate")
        w_val = held.tile([P, H * C], BF16, name="w_val")
        offsets = held.tile([P, N // 16], U16, name="offsets")
        ape_sb = held.tile([P, BLOCKS, H * R], F32, name="ape_sb")
        gain = held.tile([P, BLOCKS, 1], F32, name="gain")
        window = [held.tile([P, SLOTS], F32, name=f"window{b}") for b in range(BLOCKS)]
        nc.sync.dma_start(x_sb[:], x)
        nc.scalar.dma_start(w_gate[:], w[:, H * C : 2 * H * C])
        nc.sync.dma_start(w_val[:], w[:, 0 : H * C])
        nc.scalar.dma_start(ape_sb[:], ape.rearrange("(b p) k -> p b k", p=P))
        nc.scalar.dma_start(gain[:], norm_weight.rearrange("(b p) o -> p b o", p=P))
        nc.sync.dma_start(offsets[:], offs)
        for b in range(BLOCKS):
            nc.sync.dma_start(window[b][:], base[b * P : (b + 1) * P, :])

        ones = held.tile([P, P], F32, name="ones")
        nc.gpsimd.memset(ones[:], 1.0)

        identity = held.tile([P, P], F32, name="identity")
        make_identity(nc, identity[:])

        x_by_place = x_sb[:].rearrange("k (j r) -> k r j", r=R)

        units = [(b, h) for b in range(BLOCKS) for h in range(H)]
        def project(name, weights, unit, places):
            b, h = unit
            bank = banks.tile([P, len(places), N], F32, name=f"{name}{b}{h}{places[0]}", tag="bank")
            nc.tensor.matmul(
                bank[:],
                weights[:, h * C + b * P : h * C + (b + 1) * P],
                x_by_place[:, places[0] : places[-1] + 1, :],
                start=True,
                stop=True,
            )
            return bank

        all_places = range(R)
        halves = (range(0, R // 2), range(R // 2, R))
        gate_ps = {unit: project("gate_ps", w_gate, unit, all_places) for unit in units[:GATES_AHEAD]}
        val_ps = {}
        for i, unit in enumerate(units):
            if i + GATES_AHEAD < len(units):
                gate_ps[units[i + GATES_AHEAD]] = project("gate_ps", w_gate, units[i + GATES_AHEAD], all_places)
            val_ps[unit] = [project("val_ps", w_val, unit, half) for half in halves]

        comp = []
        squares = []
        for b in range(BLOCKS):
            terms = held.tile([P, H * R, N], F32, name=f"terms{b}")
            nc.vector.memset(terms[:, R : H * R, 0:1], 0.0)
            on_tensor = b < BLOCKS - 1
            if on_tensor:
                comp_ps = banks.tile([P, N], F32, name="comp_ps", tag="bank")
            for h in range(H):
                sig = held.tile([P, R, N], F32, name=f"sig{b}{h}")
                nc.scalar.activation(sig[:], gate_ps[b, h][:], SIGMOID)
                for r in range(R):
                    half = val_ps[b, h][r // (R // 2)]
                    nc.vector.scalar_tensor_tensor(
                        out=terms[:, h * R + r, h:N],
                        in0=half[:, r % (R // 2), 0 : N - h],
                        scalar=ape_sb[:, b, h * R + r : h * R + r + 1],
                        in1=sig[:, r, 0 : N - h],
                        op0=MULT,
                        op1=MULT,
                    )
                if on_tensor:
                    first, middle, end = h * R, h * R + R // 2, (h + 1) * R
                    pairs = held.tile([P, R // 2, N], F32, name=f"pairs{h}")
                    nc.gpsimd.tensor_tensor(pairs[:], terms[:, first:middle, :], terms[:, middle:end, :], ADD)
                    for i in range(R // 2):
                        nc.tensor.matmul(
                            comp_ps[:],
                            identity[:],
                            pairs[:, i, :],
                            start=(h == 0 and i == 0),
                            stop=(h == H - 1 and i == R // 2 - 1),
                        )
            squares_b = held.tile([P, N], F32, name=f"squares{b}")
            if on_tensor:
                comp_b = comp_ps
                nc.scalar.activation(squares_b[:], comp_b[:], SQUARE)
            else:
                comp_b = held.tile([P, N], F32, name="comp_sb")
                places = held.tile([P, R, N], F32, name="places")
                for half in halves:
                    first, end = half[0], half[-1] + 1
                    nc.vector.tensor_tensor(
                        places[:, first:end, :], terms[:, first:end, :], terms[:, R + first : R + end, :], ADD
                    )
                two = held.tile([P, R // 2, N], F32, name="two")
                nc.vector.tensor_tensor(two[:], places[:, 0 : R // 2, :], places[:, R // 2 : R, :], ADD)
                nc.vector.tensor_tensor(comp_b[:], two[:, 0, :], two[:, 1, :], ADD)
                nc.vector.tensor_tensor(squares_b[:], comp_b[:], comp_b[:], MULT)
            comp.append(comp_b)
            squares.append(squares_b)

        early_call = held.tile([P, 1], F32, name="early_call")
        nc.scalar.activation(early_call[:], sig[:, 0, 0:1], RSQRT, bias=1.0)

        square_sum = banks.tile([P, N], F32, name="square_sum", tag="bank")
        for b in range(BLOCKS):
            nc.tensor.matmul(square_sum[:], ones[:], squares[b][:], start=(b == 0), stop=(b == BLOCKS - 1))

        rms = held.tile([P, N], F32, name="rms")
        nc.scalar.activation(rms[:], square_sum[:], RSQRT, bias=EPS, scale=1.0 / C)

        scaled = []
        for b in range(BLOCKS):
            comp_gain = held.tile([P, N], F32, name=f"comp_gain{b}")
            nc.vector.tensor_scalar(out=comp_gain[:], in0=comp[b][:], scalar1=gain[:, b, :], scalar2=None, op0=MULT)
            scaled.append(comp_gain)

        for b, queue in zip(range(BLOCKS), (nc.sync, nc.scalar)):
            nc.vector.tensor_tensor(window[b][:].indirect(offsets[:]), scaled[b][:], rms[:], MULT)
            queue.dma_start(out[b * P : (b + 1) * P, :], window[b][:])
